import numpy as np
import ml_dtypes


def mxq(x, axis, fmt="e4m3"):
    dtype, down = {"e4m3": (ml_dtypes.float8_e4m3fn, 7), "e5m2": (ml_dtypes.float8_e5m2, 14)}[fmt]
    v = np.moveaxis(np.asarray(x, np.float32).astype(ml_dtypes.bfloat16).astype(np.float64), axis, -1)
    blocks = v.reshape(v.shape[:-1] + (-1, 32))
    amax = np.abs(blocks).max(-1, keepdims=True)
    byte = np.maximum(np.where(amax > 0, np.frexp(amax)[1] - 1 + 127, 0) - down, 1)
    scale = np.exp2(byte - 127.0)
    codes = (blocks / scale).astype(np.float32).astype(dtype).astype(np.float64)
    return np.moveaxis((codes * scale).reshape(v.shape), -1, axis)


WIDE = False


def mx_kscale(k):
    if not WIDE:
        return np.ones(k)
    levels = np.array([18, -18])
    if k % 512:
        return np.exp2(np.random.permutation(np.resize(levels, k // 32))).repeat(32)
    a = np.empty((k // 512, 16))
    for p in range(k // 512):
        a[p, :8] = np.random.permutation(np.resize(levels, 8))
        for g in range(8):
            far = levels[np.abs(levels - a[p, g]) >= 10]
            a[p, g + 8] = far[np.random.randint(len(far))]
    return np.exp2(a.ravel()).repeat(32)


BF16 = ml_dtypes.bfloat16


def bf(x):
    return np.asarray(x, np.float32).astype(BF16)


def f64(x):
    return np.asarray(x).astype(np.float64)


B, C_IN, H, W, HID, K, C_OUT = 2, 1024, 16, 32, 512, 8, 512
T = B * H * W


def by_token(a):
    return a.transpose(1, 0, 2, 3).reshape(a.shape[1], T)


def project_in(x, w_in, b_in):
    y = f64(w_in) @ f64(x).reshape(B, C_IN, H * W)
    return y.reshape(B, HID, H, W) + f64(b_in)[None, :, None, None]


def setup_inputs():
    s = mx_kscale(T).reshape(B, 1, H, W)
    u = mx_kscale(C_OUT)
    v = mx_kscale(HID)
    x0 = bf(np.random.standard_normal((B, C_IN, H, W)))
    w0 = bf(np.random.standard_normal((HID, C_IN)) / np.sqrt(C_IN))
    b_in = bf(np.random.standard_normal(HID) * 0.3)
    centers = bf(np.linspace(-2.0, 2.0, K).reshape(1, 1, K, 1, 1) + 0.1 * np.random.standard_normal((1, HID, K, 1, 1)))
    log_widths = bf(np.random.standard_normal((1, HID, K, 1, 1)) * 0.3)
    ow0 = bf(np.random.standard_normal((C_OUT, HID, K)) * 2.0 / np.sqrt(HID * K))
    out_bias = bf(np.random.standard_normal(C_OUT) * 0.3)
    g = np.random.standard_normal((B, C_OUT, H, W)) * np.exp2(np.random.randint(-6, 1, (B, 1, H, W))) * 2.0
    z = project_in(x0, w0, b_in)
    return {
        "x": bf(f64(x0) * s),
        "w_in": bf(f64(w0) / v[:, None]),
        "b_in": b_in,
        "centers": centers,
        "log_widths": log_widths,
        "out_weight": bf(f64(ow0) * v[None, :, None] / u[:, None, None]),
        "out_bias": out_bias,
        "z": np.asarray(z, np.float32),
        "grad_out": bf(g / s * u[None, :, None, None]),
    }


def reference(x, w_in, b_in, centers, log_widths, out_weight, out_bias, z, grad_out):
    gq = mxq(by_token(f64(grad_out)), 0, "e5m2")
    owq = mxq(f64(out_weight).reshape(C_OUT, HID * K), 0, "e4m3")
    dphi = (owq.T @ gq).reshape(HID, K, T)
    zf = by_token(f64(z))[:, None, :]
    cen = f64(centers).reshape(HID, K, 1)
    widths = np.logaddexp(f64(log_widths), 0.0).reshape(HID, K, 1) + 1e-4
    a = (zf - cen) / widths
    dz = (dphi * (np.exp(-(a ** 2)) * (-2.0 * a / widths))).sum(axis=1)
    dx = mxq(f64(w_in), 0, "e4m3").T @ mxq(dz, 0, "e5m2")
    dx = dx.reshape(C_IN, B, H, W).transpose(1, 0, 2, 3)
    dw = mxq(dz, 1, "e5m2") @ mxq(by_token(f64(x)), 1, "e4m3").T
    return dx, dw

@@ -1,0 +1,526 @@
+from contextlib import ExitStack
+
+import concourse.mybir as mybir
+from concourse.masks import make_identity
+
+F32 = mybir.dt.float32
+BF16 = mybir.dt.bfloat16
+U32 = mybir.dt.uint32
+U8 = mybir.dt.uint8
+E4 = mybir.dt.float8_e4m3fn_x4
+E5 = mybir.dt.float8_e5m2_x4
+ACT = mybir.ActivationFunctionType
+ALU = mybir.AluOpType
+
+B, C_IN, HW, HID, K, C_OUT = 2, 1024, 512, 512, 8, 512
+FLOPS = 2 * C_OUT * HID * K * B * HW + 2 * 2 * HID * C_IN * B * HW
+
+P = 128
+SLOTS = 4
+UPS = 4
+IND = (0, 1, 2, 4, 5, 6)
+
+
+def tile_rbfkanhead_v_kernel(
+    tc, x, w_in, b_in, centers, log_widths, out_weight, out_bias, z, grad_out, dx, dw
+):
+    nc = tc.nc
+    z_v = z.rearrange("b (m t) h w -> b m t (h w)", t=SLOTS)
+    g_v = grad_out.rearrange("b (p j) h w -> b p j (h w)", j=SLOTS)
+    ow_v = out_weight.rearrange("(p j) c k -> p j (c k)", j=SLOTS)
+    w_v = w_in.rearrange("(p j) i -> p j i", j=SLOTS)
+    x_v = x.rearrange("b (n p) h w -> b p n (h w)", p=P)
+    dx_v = dx.rearrange("b (m n) h w -> b m n (h w)", n=8)
+    dw_v = dw.rearrange("(m t) i -> m t i", t=SLOTS)
+
+    with ExitStack() as ctx:
+        keep = ctx.enter_context(tc.tile_pool(name="keep", bufs=1))
+        raw8 = ctx.enter_context(tc.tile_pool(name="raw8", bufs=5))
+        grp8 = ctx.enter_context(tc.tile_pool(name="grp8", bufs=3))
+        raw4 = ctx.enter_context(tc.tile_pool(name="raw4", bufs=2))
+        grp4 = ctx.enter_context(tc.tile_pool(name="grp4", bufs=3))
+        zpool = ctx.enter_context(tc.tile_pool(name="zpool", bufs=4))
+        zperm = ctx.enter_context(tc.tile_pool(name="zperm", bufs=3))
+        ztpool = ctx.enter_context(tc.tile_pool(name="ztpool", bufs=2))
+        epool = ctx.enter_context(tc.tile_pool(name="epool", bufs=9))
+        ppool = ctx.enter_context(tc.tile_pool(name="ppool", bufs=7))
+        qpool = ctx.enter_context(tc.tile_pool(name="qpool", bufs=7))
+        spool = ctx.enter_context(tc.tile_pool(name="spool", bufs=4))
+        mm = ctx.enter_context(tc.psum_pool(name="mm", bufs=4))
+        acc = ctx.enter_context(tc.psum_pool(name="acc", bufs=2))
+        ctx.enter_context(tc.manual_schedule())
+
+        lw_t = keep.tile([P, SLOTS * K], BF16, name="lw_t")
+        cen_t = keep.tile([P, SLOTS * K], BF16, name="cen_t")
+        nc.sync.dma_start(out=lw_t[:], in_=log_widths.rearrange("a (m t) k b c -> m (a t k b c)", t=SLOTS))
+        nc.sync.dma_start(out=cen_t[:], in_=centers.rearrange("a (m t) k b c -> m (a t k b c)", t=SLOTS))
+        z_raw = {}
+
+        def load_z(g, t):
+            zt_ = zpool.tile([P, HW], F32, name="z_raw", tag="z_raw")
+            nc.sync.dma_start(out=zt_[:], in_=z_v[g, :, t, :])
+            z_raw[g, t] = zt_
+
+        def load_g(g):
+            gt_ = raw4.tile([P, SLOTS, HW], BF16, name="g_raw", tag="g_raw")
+            nc.sync.dma_start(out=gt_[:], in_=g_v[g])
+            return gt_
+
+        load_z(0, 0)
+        g_raw = {0: load_g(0)}
+        ow_raw = []
+        for q in range(4):
+            r = raw8.tile([P, SLOTS, 1024], BF16, name="ow_raw", tag="raw8")
+            nc.sync.dma_start(out=r[:], in_=ow_v[:, :, 1024 * q : 1024 * (q + 1)])
+            ow_raw.append(r)
+        load_z(0, 1)
+        load_z(0, 2)
+        load_z(0, 3)
+        w_raw = raw8.tile([P, SLOTS, C_IN], BF16, name="w_raw", tag="raw8")
+        nc.sync.dma_start(out=w_raw[:], in_=w_v)
+        g_raw[1] = load_g(1)
+        x_raw = {}
+
+        def load_x(b):
+            xt_ = raw8.tile([P, 8, HW], BF16, name="x_raw", tag="raw8")
+            nc.sync.dma_start(out=xt_[:], in_=x_v[b])
+            x_raw[b] = xt_
+
+        ident = keep.tile([P, P], F32, name="ident")
+        make_identity(nc, ident[:])
+        ab = keep.tile([P, SLOTS * K], F32, name="ab")
+        ex = keep.tile([P, SLOTS * K], F32, name="ex")
+        l1 = keep.tile([P, SLOTS * K], F32, name="l1")
+        wd = keep.tile([P, SLOTS * K], F32, name="wd")
+        inv = keep.tile([P, SLOTS * K], F32, name="inv")
+        sq = keep.tile([P, SLOTS * K], F32, name="sq")
+        nsq = keep.tile([P, SLOTS * K], F32, name="nsq")
+        alpha = keep.tile([P, SLOTS * K], F32, name="alpha")
+        negc = keep.tile([P, SLOTS * K], F32, name="negc")
+
+        nc.scalar.activation(ab[:], lw_t[:], ACT.Abs)
+        nc.scalar.activation(ex[:], ab[:], ACT.Exp, scale=-1.0)
+        nc.scalar.activation(l1[:], ex[:], ACT.Ln, bias=1.0)
+
+        nc.vector.tensor_scalar(negc[:], cen_t[:], -1.0, None, ALU.mult)
+
+        z_perm = {}
+
+        def permute_z(engine, g, t):
+            zp = zperm.tile([P, HW], F32, name="zp", tag="zp")
+            dst = zp[:].rearrange("c (j p) -> c j p", j=SLOTS)
+            src = z_raw[g, t][:].rearrange("c (p j) -> c j p", j=SLOTS)
+            if engine is nc.vector:
+                nc.vector.tensor_copy(out=dst, in_=src)
+            else:
+                engine.tensor_scalar(dst, src, 1.0, 1.0, ALU.mult, ALU.mult)
+            z_perm[g, t] = zp
+
+        permute_z(nc.vector, 0, 0)
+        nc.vector.scalar_tensor_tensor(wd[:], lw_t[:], 0.0, l1[:], ALU.max, ALU.add)
+        nc.vector.tensor_scalar(wd[:], wd[:], 1e-4, None, ALU.add)
+        nc.vector.reciprocal(inv[:], wd[:])
+        nc.vector.tensor_tensor(sq[:], inv[:], inv[:], ALU.mult)
+        nc.vector.tensor_scalar(nsq[:], sq[:], -1.0, None, ALU.mult)
+        nc.vector.tensor_scalar(alpha[:], sq[:], -2.0, None, ALU.mult)
+
+        def quant(codes, scales, src, fmt):
+            nc.vector.quantize_mx(out=codes.bitcast(fmt), scales=scales, in_=src)
+
+        def interleave(engine, dst, src):
+            if engine is nc.vector:
+                nc.vector.tensor_copy(out=dst, in_=src)
+            elif engine is nc.scalar:
+                nc.scalar.copy(dst, src)
+            else:
+                engine.tensor_scalar(dst, src, 1.0, 1.0, ALU.mult, ALU.mult)
+
+        gq, gs = {}, {}
+        g_grp = {}
+
+        def group_g(engine, g):
+            gg = grp4.tile([P, HW * SLOTS], BF16, name="gg", tag="grp4", align_bytes=64)
+            interleave(
+                engine,
+                gg[:].rearrange("p (b a j) -> p b a j", b=SLOTS, j=SLOTS),
+                g_raw[g][:].rearrange("p j (a b) -> p b a j", b=SLOTS),
+            )
+            g_grp[g] = gg
+
+        def quant_g(g):
+            gq[g] = keep.tile([P, HW], U32, name=f"gq{g}", align_bytes=64)
+            gs[g] = keep.tile([P, HW], U8, name=f"gs{g}", align_bytes=64)
+            quant(gq[g][:], gs[g][:], g_grp[g][:], E5)
+
+        ow_grp, oq, osc = {}, {}, {}
+
+        def group_ow(engine, t, q):
+            if t not in ow_grp:
+                ow_grp[t] = grp8.tile([P, K, P, SLOTS], BF16, name="ow_grp", tag="grp8", align_bytes=64)
+            interleave(
+                engine,
+                ow_grp[t][:, :, 32 * q : 32 * (q + 1), :],
+                ow_raw[q][:].rearrange("p j (m t k) -> p t k m j", t=SLOTS, k=K)[:, t],
+            )
+
+        def quant_ow(t, half):
+            if t not in oq:
+                oq[t] = keep.tile([P, K * P], U32, name=f"oq{t}", align_bytes=64)
+                osc[t] = keep.tile([P, K * P], U8, name=f"os{t}", align_bytes=64)
+            cols = slice(half * 512, half * 512 + 512)
+            src = ow_grp[t][:].rearrange("p k m j -> p (k m j)")[:, half * 2048 : half * 2048 + 2048]
+            quant(oq[t][:, cols], osc[t][:, cols], src, E4)
+
+        w_grp = {}
+        wq = keep.tile([P, C_IN], U32, name="wq", align_bytes=64)
+        ws = keep.tile([P, C_IN], U8, name="ws", align_bytes=64)
+
+        def group_w(engine, n0):
+            if 0 not in w_grp:
+                w_grp[0] = grp8.tile([P, 8, P, SLOTS], BF16, name="w_grp", tag="grp8", align_bytes=64)
+            interleave(
+                engine,
+                w_grp[0][:, n0 : n0 + 2],
+                w_raw[:].rearrange("p j (m n) -> p n m j", n=8)[:, n0 : n0 + 2],
+            )
+
+        def quant_w():
+            quant(wq[:], ws[:], w_grp[0][:].rearrange("p n m j -> p (n m j)"), E4)
+
+        xq = {b: keep.tile([P, C_IN], U32, name=f"xq{b}", align_bytes=64) for b in range(B)}
+        xs = {b: keep.tile([P, C_IN], U8, name=f"xs{b}", align_bytes=64) for b in range(B)}
+        x_grp, x_bank = {}, {}
+
+        def turn_x(i):
+            b, q = i // 4, i % 4
+            bank = mm.tile([P, 2, 256], F32, name="x_bank", tag="mm")
+            for a in range(2):
+                words = x_raw[b][:, 2 * q + a, :].bitcast(F32).rearrange("i (p u) -> i p u", u=2)
+                for u in range(2):
+                    nc.tensor.transpose(bank[:, u, P * a : P * (a + 1)], words[:, :, u], ident[:])
+            x_bank[i] = bank
+
+        def copy_x(i):
+            if i % 2 == 0:
+                x_grp[i // 2] = grp4.tile([P, 512 * SLOTS], BF16, name="x_grp", tag="grp4", align_bytes=64)
+            dst = x_grp[i // 2][:, 1024 * (i % 2) : 1024 * (i % 2 + 1)].bitcast(F32)
+            nc.vector.tensor_copy(
+                out=dst.rearrange("p (i u) -> p i u", u=2), in_=x_bank[i][:].rearrange("p u i -> p i u")
+            )
+
+        def quant_x(i):
+            b, half = i // 2, i % 2
+            cols = slice(512 * half, 512 * (half + 1))
+            quant(xq[b][:, cols], xs[b][:, cols], x_grp[i][:], E4)
+
+        es, ps, qs, dphi = {}, {}, {}, {}
+
+        def split(n):
+            return n // 32, (n // 8) % 4, n % 8
+
+        def gauss(n):
+            g, t, k = split(n)
+            col = t * K + k
+            e = epool.tile([P, HW], F32, name="e", tag="e")
+            nc.scalar.activation(e[:], z_perm[g, t][:], ACT.Square, bias=negc[:, col : col + 1])
+            nc.scalar.activation(e[:], e[:], ACT.Exp, scale=nsq[:, col : col + 1])
+            es[n] = e
+
+        def mx_dphi(n):
+            g, t, k = split(n)
+            bank = mm.tile([P, HW], F32, name="dphi", tag="mm")
+            nc.tensor.matmul_mx(
+                out=bank[:],
+                lhsT=oq[t][:, k * P : (k + 1) * P].bitcast(E4),
+                lhsT_scale=osc[t][:, k * P : (k + 1) * P],
+                rhs=gq[g][:].bitcast(E5),
+                rhs_scale=gs[g][:],
+                start=True,
+                stop=True,
+            )
+            dphi[n] = bank
+
+        def offset(n):
+            g, t, k = split(n)
+            col = t * K + k
+            if k not in IND:
+                nc.vector.scalar_tensor_tensor(
+                    es[n][:], z_perm[g, t][:], negc[:, col : col + 1], es[n][:], ALU.add, ALU.mult
+                )
+
+        def product(n):
+            g, t, k = split(n)
+            col = t * K + k
+            p = ppool.tile([P, HW], F32, name="p", tag="p")
+            nc.vector.scalar_tensor_tensor(
+                p[:], dphi[n][:], alpha[:, col : col + 1], es[n][:], ALU.mult, ALU.mult
+            )
+            ps[n] = p
+
+        def times_center(n):
+            g, t, k = split(n)
+            col = t * K + k
+            if k in IND:
+                q = qpool.tile([P, HW], F32, name="q", tag="q")
+                nc.gpsimd.tensor_scalar(q[:], ps[n][:], negc[:, col : col + 1], 1.0, ALU.mult, ALU.mult)
+                qs[n] = q
+
+        bank1, bank2 = {}, {}
+
+        def add_turned(bank, src, first, last):
+            for j in range(SLOTS):
+                nc.tensor.matmul(
+                    bank[:, j, :],
+                    src[:, P * j : P * (j + 1)],
+                    ident[:],
+                    start=first and j == 0,
+                    stop=last and j == SLOTS - 1,
+                    is_transpose=True,
+                )
+
+        def sums(n):
+            g, t, k = split(n)
+            blk = n // 8
+            if k == 0:
+                bank2[blk] = acc.tile([P, SLOTS, P], F32, name="bank2", tag="bank2")
+                bank1[blk] = acc.tile([P, SLOTS, P], F32, name="bank1", tag="bank1")
+            if k in IND:
+                add_turned(bank1[blk], ps[n], k == IND[0], k == IND[-1])
+            add_turned(bank2[blk], qs[n] if k in IND else ps[n], k == 0, k == K - 1)
+
+        zt_bank, zts = {}, {}
+
+        def turn_z(blk):
+            bank = mm.tile([P, SLOTS, P], F32, name="zt_bank", tag="mm")
+            for j in range(SLOTS):
+                nc.tensor.transpose(bank[:, j, :], z_perm[blk // 4, blk % 4][:, P * j : P * (j + 1)], ident[:])
+            zt_bank[blk] = bank
+
+        def copy_z(blk):
+            zt = ztpool.tile([P, P, SLOTS], F32, name="zt", tag="zt")
+            nc.vector.tensor_copy(out=zt[:], in_=zt_bank[blk][:].rearrange("p j m -> p m j"))
+            zts[blk] = zt
+
+        ys, dz = {}, {}
+        tq = {b: keep.tile([P, SLOTS * P], U32, name=f"tq{b}", align_bytes=64) for b in range(B)}
+        tsc = {b: keep.tile([P, SLOTS * P], U8, name=f"tsc{b}", align_bytes=64) for b in range(B)}
+        for b in range(B):
+            dz[b] = keep.tile([P, SLOTS, P * SLOTS], BF16, name=f"dz{b}", align_bytes=64)
+
+        def finish_a(blk):
+            y = ztpool.tile([P, P, SLOTS], F32, name="y", tag="y")
+            nc.vector.tensor_tensor(y[:], bank1[blk][:].rearrange("p j m -> p m j"), zts[blk][:], ALU.mult)
+            ys[blk] = y
+
+        def finish_b(blk):
+            dst = dz[blk // 4][:, blk % 4, :].rearrange("p (m j) -> p m j", j=SLOTS)
+            nc.vector.tensor_tensor(dst, bank2[blk][:].rearrange("p j m -> p m j"), ys[blk][:], ALU.add)
+
+        def quant_t(blk):
+            g, t = blk // 4, blk % 4
+            cols = slice(P * t, P * (t + 1))
+            quant(tq[g][:, cols], tsc[g][:, cols], dz[g][:, t, :], E5)
+
+        back_bank = {}
+
+        def turn_back(g, ts):
+            for u in range(2):
+                if (g, u) not in back_bank:
+                    back_bank[g, u] = mm.tile([P, SLOTS, P], F32, name="back", tag="mm")
+                for t in ts:
+                    words = dz[g][:, t, :].bitcast(F32).rearrange("p (m u) -> p m u", u=2)
+                    nc.tensor.transpose(back_bank[g, u][:, t, :], words[:, :, u], ident[:])
+
+        dzc, cq, cs = {}, {}, {}
+
+        def copy_back(g, u, engine):
+            if u == 0:
+                dzc[g] = grp4.tile([P, HW * SLOTS], BF16, name="dzc", tag="grp4", align_bytes=64)
+            src = back_bank[g, u][:].rearrange("m t p -> m (t p)").bitcast(BF16)
+            src = src.rearrange("m (t p e) -> m p e t", t=SLOTS, e=2)
+            dst = dzc[g][:].rearrange("m (p u e t) -> m u p e t", u=2, e=2, t=SLOTS)[:, u]
+            copy_out(engine, dst, src)
+
+        def copy_out(engine, dst, src):
+            if engine is nc.vector:
+                nc.vector.tensor_copy(out=dst, in_=src)
+            else:
+                nc.scalar.copy(dst, src)
+
+        def quant_c(g):
+            cq[g] = keep.tile([P, HW], U32, name=f"cq{g}", align_bytes=64)
+            cs[g] = keep.tile([P, HW], U8, name=f"cs{g}", align_bytes=64)
+            quant(cq[g][:], cs[g][:], dzc[g][:], E5)
+
+        stage = {}
+
+        out_bank = {}
+
+        def mx_dx(g, n):
+            bank = mm.tile([P, HW], F32, name="dx_bank", tag="mm")
+            nc.tensor.matmul_mx(
+                out=bank[:],
+                lhsT=wq[:, P * n : P * (n + 1)].bitcast(E4),
+                lhsT_scale=ws[:, P * n : P * (n + 1)],
+                rhs=cq[g][:].bitcast(E5),
+                rhs_scale=cs[g][:],
+                start=True,
+                stop=True,
+            )
+            out_bank["x", g, n] = bank
+
+        def copy_dx(g, n, engine):
+            if n % 2 == 0:
+                stage["x", g, n // 2] = spool.tile([P, 2, HW], F32, name="stage", tag="stage")
+            st = stage["x", g, n // 2]
+            copy_out(engine, st[:, n % 2, :], out_bank["x", g, n][:])
+            if n % 2 == 1:
+                nc.sync.dma_start(out=dx_v[g, :, n - 1 : n + 1, :], in_=st[:])
+
+        def mx_dw(t, half):
+            bank = mm.tile([P, 512], F32, name="dw_bank", tag="mm")
+            for g in range(B):
+                nc.tensor.matmul_mx(
+                    out=bank[:],
+                    lhsT=tq[g][:, P * t : P * (t + 1)].bitcast(E5),
+                    lhsT_scale=tsc[g][:, P * t : P * (t + 1)],
+                    rhs=xq[g][:, 512 * half : 512 * (half + 1)].bitcast(E4),
+                    rhs_scale=xs[g][:, 512 * half : 512 * (half + 1)],
+                    start=g == 0,
+                    stop=g == B - 1,
+                )
+            out_bank["w", t, half] = bank
+
+        def copy_dw(t, half, engine):
+            if half == 0:
+                stage["w", t] = spool.tile([P, 2, 512], F32, name="stage", tag="stage")
+            st = stage["w", t]
+            copy_out(engine, st[:, half, :], out_bank["w", t, half][:])
+            if half == 1:
+                nc.sync.dma_start(out=dw_v[:, t, :], in_=st[:].rearrange("m h i -> m (h i)"))
+
+        group_g(nc.vector, 0)
+        quant_g(0)
+        for q in range(3):
+            group_ow(nc.vector, 0, q)
+            group_ow(nc.vector, 2, q)
+        group_ow(nc.vector, 0, 3)
+        quant_ow(0, 0)
+        quant_ow(0, 1)
+
+        n_steps = 64 // UPS
+        pe_turn = {}
+        pe_mx = {}
+        vec = {}
+        gp = {}
+
+        def at(table, s, fn, *args):
+            table.setdefault(s, []).append((fn, args))
+
+        V = nc.vector
+        S = nc.scalar
+        G = nc.gpsimd
+        at(vec, 0, group_ow, V, 2, 3)
+        at(vec, 1, quant_ow, 1, 0)
+        at(vec, 1, quant_ow, 1, 1)
+        at(vec, 2, quant_ow, 2, 0)
+        at(vec, 2, quant_ow, 2, 1)
+        at(vec, 4, quant_ow, 3, 0)
+        at(vec, 4, quant_ow, 3, 1)
+        at(gp, -1, permute_z, G, 0, 1)
+        for q in range(4):
+            at(gp, 0 if q < 2 else 1, group_ow, G, 3, q)
+        at(gp, 1, permute_z, G, 0, 2)
+        at(gp, 2, load_x, 0)
+        at(gp, 2, group_g, G, 1)
+        at(gp, 3, permute_z, G, 0, 3)
+        at(gp, 3, load_x, 1)
+        for g1t in range(4):
+            at(gp, 3 + g1t, load_z, 1, g1t)
+        for n0 in range(4):
+            at(gp, 3 + n0 // 2, group_w, G, 2 * n0)
+        at(gp, 5, permute_z, G, 1, 0)
+        at(gp, 7, permute_z, G, 1, 1)
+        at(gp, 9, permute_z, G, 1, 2)
+        at(gp, 11, permute_z, G, 1, 3)
+        at(vec, 5, quant_g, 1)
+        at(vec, 6, quant_w)
+        for i in range(8):
+            at(pe_turn, 3 + i, turn_x, i)
+            at(vec, 3 + i, copy_x, i)
+            if i % 2 == 1:
+                at(vec, 4 + i, quant_x, i // 2)
+        for blk in range(8):
+            at(pe_turn, 2 * blk + 1, turn_z, blk)
+            at(vec, 2 * blk + 1, copy_z, blk)
+            at(vec, 2 * blk + 2, finish_a, blk)
+        for blk in range(8):
+            at(vec, 2 * blk + 2, finish_b, blk)
+            at(vec, 2 * blk + 3 if blk < 7 else 16, quant_t, blk)
+        at(pe_turn, 9, turn_back, 0, range(4))
+        at(vec, 9, copy_back, 0, 0, V)
+        at(vec, 9, copy_back, 0, 1, V)
+        at(vec, 10, quant_c, 0)
+        for n in range(8):
+            at(pe_mx, 11 + n // 2, mx_dx, 0, n)
+            at(vec, 11 + n // 2, copy_dx, 0, n, V)
+        for t in range(2):
+            for half in range(2):
+                at(pe_mx, 12 + 2 * t, mx_dw, t, half)
+                at(vec, 12 + 2 * t, copy_dw, t, half, V)
+
+        def run(fns):
+            for fn, args in fns:
+                fn(*args)
+
+        run(gp.get(-1, []))
+        for s in range(n_steps + 1):
+            units = range(UPS * s, UPS * (s + 1)) if s < n_steps else range(0)
+            for n in units:
+                gauss(n)
+                if s == 1:
+                    group_ow(S, 1, n - UPS)
+            for n in units:
+                mx_dphi(n)
+            run(pe_mx.get(s, []))
+            if s > 0:
+                for n in range(UPS * (s - 1), UPS * s):
+                    sums(n)
+            run(pe_turn.get(s, []))
+            turned = (copy_x, copy_z, copy_back)
+            copies = (copy_dx, copy_dw)
+            last = [f for f in vec.get(s, []) if f[0] in turned]
+            todo = [f for f in vec.get(s, []) if f[0] in copies]
+            todo = todo + [f for f in vec.get(s, []) if f[0] not in copies and f[0] not in turned]
+            for n in units:
+                if n == UPS * s:
+                    offset(n)
+                if n + 1 in units:
+                    offset(n + 1)
+                product(n)
+                times_center(n)
+                if len(todo) > 0:
+                    run(todo[:1])
+                    todo = todo[1:]
+            run(todo)
+            run(last)
+            run(gp.get(s, []))
+
+        for half in range(2):
+            mx_dw(2, half)
+        turn_back(1, range(4))
+        copy_back(1, 0, S)
+        copy_back(1, 1, V)
+        for half in range(2):
+            copy_dw(2, half, S)
+        quant_c(1)
+        for n in range(2):
+            mx_dx(1, n)
+        for n in range(8):
+            copy_dx(1, n, V if n % 2 == 0 else S)
+            if n + 2 < 8:
+                mx_dx(1, n + 2)
+        for half in range(2):
+            mx_dw(3, half)
+        copy_dw(3, 0, V)
+        copy_dw(3, 1, S)

@@ -18,7 +18,6 @@ FLOPS = 2 * C_OUT * HID * K * B * HW + 2 * 2 * HID * C_IN * B * HW
 P = 128
 SLOTS = 4
 UPS = 4
-IND = (0, 1, 2, 4, 5, 6)
 
 
 def tile_rbfkanhead_v_kernel(
@@ -41,12 +40,10 @@ def tile_rbfkanhead_v_kernel(
         grp4 = ctx.enter_context(tc.tile_pool(name="grp4", bufs=3))
         zpool = ctx.enter_context(tc.tile_pool(name="zpool", bufs=4))
         zperm = ctx.enter_context(tc.tile_pool(name="zperm", bufs=3))
-        ztpool = ctx.enter_context(tc.tile_pool(name="ztpool", bufs=2))
         epool = ctx.enter_context(tc.tile_pool(name="epool", bufs=9))
-        ppool = ctx.enter_context(tc.tile_pool(name="ppool", bufs=7))
-        qpool = ctx.enter_context(tc.tile_pool(name="qpool", bufs=7))
+        ppool = ctx.enter_context(tc.tile_pool(name="ppool", bufs=9))
         spool = ctx.enter_context(tc.tile_pool(name="spool", bufs=4))
-        mm = ctx.enter_context(tc.psum_pool(name="mm", bufs=4))
+        mm = ctx.enter_context(tc.psum_pool(name="mm", bufs=6))
         acc = ctx.enter_context(tc.psum_pool(name="acc", bufs=2))
         ctx.enter_context(tc.manual_schedule())
 
@@ -200,13 +197,11 @@ def tile_rbfkanhead_v_kernel(
                     nc.tensor.transpose(bank[:, u, P * a : P * (a + 1)], words[:, :, u], ident[:])
             x_bank[i] = bank
 
-        def copy_x(i):
+        def copy_x(i, engine):
             if i % 2 == 0:
                 x_grp[i // 2] = grp4.tile([P, 512 * SLOTS], BF16, name="x_grp", tag="grp4", align_bytes=64)
             dst = x_grp[i // 2][:, 1024 * (i % 2) : 1024 * (i % 2 + 1)].bitcast(F32)
-            nc.vector.tensor_copy(
-                out=dst.rearrange("p (i u) -> p i u", u=2), in_=x_bank[i][:].rearrange("p u i -> p i u")
-            )
+            copy_out(engine, dst.rearrange("p (i u) -> p i u", u=2), x_bank[i][:].rearrange("p u i -> p i u"))
 
         def quant_x(i):
             b, half = i // 2, i % 2
@@ -243,10 +238,9 @@ def tile_rbfkanhead_v_kernel(
         def offset(n):
             g, t, k = split(n)
             col = t * K + k
-            if k not in IND:
-                nc.vector.scalar_tensor_tensor(
-                    es[n][:], z_perm[g, t][:], negc[:, col : col + 1], es[n][:], ALU.add, ALU.mult
-                )
+            nc.vector.scalar_tensor_tensor(
+                es[n][:], z_perm[g, t][:], negc[:, col : col + 1], es[n][:], ALU.add, ALU.mult
+            )
 
         def product(n):
             g, t, k = split(n)
@@ -257,15 +251,7 @@ def tile_rbfkanhead_v_kernel(
             )
             ps[n] = p
 
-        def times_center(n):
-            g, t, k = split(n)
-            col = t * K + k
-            if k in IND:
-                q = qpool.tile([P, HW], F32, name="q", tag="q")
-                nc.gpsimd.tensor_scalar(q[:], ps[n][:], negc[:, col : col + 1], 1.0, ALU.mult, ALU.mult)
-                qs[n] = q
-
-        bank1, bank2 = {}, {}
+        bank2 = {}
 
         def add_turned(bank, src, first, last):
             for j in range(SLOTS):
@@ -283,38 +269,18 @@ def tile_rbfkanhead_v_kernel(
             blk = n // 8
             if k == 0:
                 bank2[blk] = acc.tile([P, SLOTS, P], F32, name="bank2", tag="bank2")
-                bank1[blk] = acc.tile([P, SLOTS, P], F32, name="bank1", tag="bank1")
-            if k in IND:
-                add_turned(bank1[blk], ps[n], k == IND[0], k == IND[-1])
-            add_turned(bank2[blk], qs[n] if k in IND else ps[n], k == 0, k == K - 1)
+            add_turned(bank2[blk], ps[n], k == 0, k == K - 1)
 
-        zt_bank, zts = {}, {}
 
-        def turn_z(blk):
-            bank = mm.tile([P, SLOTS, P], F32, name="zt_bank", tag="mm")
-            for j in range(SLOTS):
-                nc.tensor.transpose(bank[:, j, :], z_perm[blk // 4, blk % 4][:, P * j : P * (j + 1)], ident[:])
-            zt_bank[blk] = bank
-
-        def copy_z(blk):
-            zt = ztpool.tile([P, P, SLOTS], F32, name="zt", tag="zt")
-            nc.vector.tensor_copy(out=zt[:], in_=zt_bank[blk][:].rearrange("p j m -> p m j"))
-            zts[blk] = zt
-
-        ys, dz = {}, {}
+        dz = {}
         tq = {b: keep.tile([P, SLOTS * P], U32, name=f"tq{b}", align_bytes=64) for b in range(B)}
         tsc = {b: keep.tile([P, SLOTS * P], U8, name=f"tsc{b}", align_bytes=64) for b in range(B)}
         for b in range(B):
             dz[b] = keep.tile([P, SLOTS, P * SLOTS], BF16, name=f"dz{b}", align_bytes=64)
 
-        def finish_a(blk):
-            y = ztpool.tile([P, P, SLOTS], F32, name="y", tag="y")
-            nc.vector.tensor_tensor(y[:], bank1[blk][:].rearrange("p j m -> p m j"), zts[blk][:], ALU.mult)
-            ys[blk] = y
-
-        def finish_b(blk):
+        def finish(blk, engine):
             dst = dz[blk // 4][:, blk % 4, :].rearrange("p (m j) -> p m j", j=SLOTS)
-            nc.vector.tensor_tensor(dst, bank2[blk][:].rearrange("p j m -> p m j"), ys[blk][:], ALU.add)
+            copy_out(engine, dst, bank2[blk][:].rearrange("p j m -> p m j"))
 
         def quant_t(blk):
             g, t = blk // 4, blk % 4
@@ -401,18 +367,13 @@ def tile_rbfkanhead_v_kernel(
 
         group_g(nc.vector, 0)
         quant_g(0)
-        for q in range(3):
+        for q in range(4):
             group_ow(nc.vector, 0, q)
-            group_ow(nc.vector, 2, q)
-        group_ow(nc.vector, 0, 3)
         quant_ow(0, 0)
         quant_ow(0, 1)
 
         n_steps = 64 // UPS
-        pe_turn = {}
-        pe_mx = {}
-        vec = {}
-        gp = {}
+        pe_turn, pe_mx, vec, sca, gp = {}, {}, {}, {}, {}
 
         def at(table, s, fn, *args):
             table.setdefault(s, []).append((fn, args))
@@ -420,54 +381,51 @@ def tile_rbfkanhead_v_kernel(
         V = nc.vector
         S = nc.scalar
         G = nc.gpsimd
-        at(vec, 0, group_ow, V, 2, 3)
-        at(vec, 1, quant_ow, 1, 0)
-        at(vec, 1, quant_ow, 1, 1)
-        at(vec, 2, quant_ow, 2, 0)
-        at(vec, 2, quant_ow, 2, 1)
-        at(vec, 4, quant_ow, 3, 0)
-        at(vec, 4, quant_ow, 3, 1)
         at(gp, -1, permute_z, G, 0, 1)
         for q in range(4):
-            at(gp, 0 if q < 2 else 1, group_ow, G, 3, q)
-        at(gp, 1, permute_z, G, 0, 2)
-        at(gp, 2, load_x, 0)
+            at(gp, -1, group_ow, G, 1, q)
+        for q in range(4):
+            at(gp, 0, group_ow, G, 2, q)
+        at(gp, 0, permute_z, G, 0, 2)
+        for q in range(4):
+            at(gp, 1, group_ow, G, 3, q)
+        at(gp, 1, permute_z, G, 0, 3)
+        at(gp, 1, load_x, 0)
         at(gp, 2, group_g, G, 1)
-        at(gp, 3, permute_z, G, 0, 3)
-        at(gp, 3, load_x, 1)
-        for g1t in range(4):
-            at(gp, 3 + g1t, load_z, 1, g1t)
+        for t in range(4):
+            at(gp, 2 + t, load_z, 1, t)
         for n0 in range(4):
             at(gp, 3 + n0 // 2, group_w, G, 2 * n0)
+        at(gp, 3, load_x, 1)
         at(gp, 5, permute_z, G, 1, 0)
         at(gp, 7, permute_z, G, 1, 1)
         at(gp, 9, permute_z, G, 1, 2)
         at(gp, 11, permute_z, G, 1, 3)
-        at(vec, 5, quant_g, 1)
+        for t in range(1, 4):
+            at(vec, 2 * t - 1, quant_ow, t, 0)
+            at(vec, 2 * t - 1, quant_ow, t, 1)
+        at(vec, 6, quant_g, 1)
         at(vec, 6, quant_w)
         for i in range(8):
             at(pe_turn, 3 + i, turn_x, i)
-            at(vec, 3 + i, copy_x, i)
+            at(sca, 5 + i, copy_x, i, S)
             if i % 2 == 1:
-                at(vec, 4 + i, quant_x, i // 2)
-        for blk in range(8):
-            at(pe_turn, 2 * blk + 1, turn_z, blk)
-            at(vec, 2 * blk + 1, copy_z, blk)
-            at(vec, 2 * blk + 2, finish_a, blk)
-        for blk in range(8):
-            at(vec, 2 * blk + 2, finish_b, blk)
-            at(vec, 2 * blk + 3 if blk < 7 else 16, quant_t, blk)
-        at(pe_turn, 9, turn_back, 0, range(4))
-        at(vec, 9, copy_back, 0, 0, V)
-        at(vec, 9, copy_back, 0, 1, V)
-        at(vec, 10, quant_c, 0)
+                at(vec, 5 + i, quant_x, i // 2)
+        for blk in range(7):
+            at(sca, 2 * blk + 4, finish, blk, S)
+            at(vec, 2 * blk + 4, quant_t, blk)
+        at(pe_turn, 10, turn_back, 0, range(4))
+        at(sca, 12, copy_back, 0, 0, S)
+        at(sca, 12, copy_back, 0, 1, S)
+        at(vec, 12, quant_c, 0)
         for n in range(8):
-            at(pe_mx, 11 + n // 2, mx_dx, 0, n)
-            at(vec, 11 + n // 2, copy_dx, 0, n, V)
+            at(pe_mx, 13 + n // 3, mx_dx, 0, n)
+            at(sca, 15 + n // 3, copy_dx, 0, n, S)
         for t in range(2):
             for half in range(2):
-                at(pe_mx, 12 + 2 * t, mx_dw, t, half)
-                at(vec, 12 + 2 * t, copy_dw, t, half, V)
+                at(pe_mx, 13 + 2 * t, mx_dw, t, half)
+                at(sca, 15 + 2 * t, copy_dw, t, half, S)
+        at(pe_mx, 16, turn_back, 1, range(3))
 
         def run(fns):
             for fn, args in fns:
@@ -475,52 +433,52 @@ def tile_rbfkanhead_v_kernel(
 
         run(gp.get(-1, []))
         for s in range(n_steps + 1):
+            ahead = list(sca.get(s + 1, []))
+            if s == 0:
+                for n in range(2 * UPS):
+                    gauss(n)
+            elif s + 1 < n_steps:
+                for n in range(UPS * (s + 1), UPS * (s + 2)):
+                    gauss(n)
             units = range(UPS * s, UPS * (s + 1)) if s < n_steps else range(0)
-            for n in units:
-                gauss(n)
-                if s == 1:
-                    group_ow(S, 1, n - UPS)
             for n in units:
                 mx_dphi(n)
             run(pe_mx.get(s, []))
-            if s > 0:
+            if 0 < s <= n_steps:
                 for n in range(UPS * (s - 1), UPS * s):
                     sums(n)
             run(pe_turn.get(s, []))
-            turned = (copy_x, copy_z, copy_back)
-            copies = (copy_dx, copy_dw)
-            last = [f for f in vec.get(s, []) if f[0] in turned]
-            todo = [f for f in vec.get(s, []) if f[0] in copies]
-            todo = todo + [f for f in vec.get(s, []) if f[0] not in copies and f[0] not in turned]
+            run(ahead)
+            todo = list(vec.get(s, []))
             for n in units:
                 if n == UPS * s:
                     offset(n)
                 if n + 1 in units:
                     offset(n + 1)
                 product(n)
-                times_center(n)
                 if len(todo) > 0:
                     run(todo[:1])
                     todo = todo[1:]
             run(todo)
-            run(last)
             run(gp.get(s, []))
 
         for half in range(2):
             mx_dw(2, half)
-        turn_back(1, range(4))
+        finish(7, V)
+        turn_back(1, (3,))
         copy_back(1, 0, S)
         copy_back(1, 1, V)
+        quant_t(7)
         for half in range(2):
             copy_dw(2, half, S)
         quant_c(1)
-        for n in range(2):
+        for half in range(2):
+            mx_dw(3, half)
+        copy_dw(3, 0, S)
+        copy_dw(3, 1, S)
+        for n in range(3):
             mx_dx(1, n)
         for n in range(8):
             copy_dx(1, n, V if n % 2 == 0 else S)
-            if n + 2 < 8:
-                mx_dx(1, n + 2)
-        for half in range(2):
-            mx_dw(3, half)
-        copy_dw(3, 0, V)
-        copy_dw(3, 1, S)
+            if n + 3 < 8:
+                mx_dx(1, n + 3)

@@ -18,6 +18,7 @@ FLOPS = 2 * C_OUT * HID * K * B * HW + 2 * 2 * HID * C_IN * B * HW
 P = 128
 SLOTS = 4
 UPS = 4
+CFG = {'gr_from': 16, 'gr_k': (2, 3, 6, 7), 'e_bufs': 12, 'ow_eng': {1: 'S', 2: 'S', 3: 'G'}, 'ow_step': {1: -1, 2: 0, 3: 2}, 'ow_per': 2, 'oq_step': {1: 0, 2: 2, 3: 4}, 'zp_lead': 5, 'zp_eng': 'G', 'x_load': 3, 'g1_eng': 'S', 'g1_step': 4, 'gq1_step': 6, 'w_eng': 'G', 'w_step': 4, 'wq_step': 10, 'x_step': 4, 'x_eng': 'S', 'fin_eng': 'V', 'back': 10, 'back_eng': 'V', 'dx_step': 13, 'dx_per': 3, 'dx_eng': 'S', 'dx_v': 1, 'dw_eng': 'S', 'defer': 0, 'mxo': 1, 'back1': 16, 'sq_k': (), 'sq_from': 16, 'd_bufs': 3, 'p_bufs': 9, 'mm': 5, 'acc': 1, 'zb': 2}
 
 
 def tile_rbfkanhead_v_kernel(
@@ -29,7 +30,7 @@ def tile_rbfkanhead_v_kernel(
     ow_v = out_weight.rearrange("(p j) c k -> p j (c k)", j=SLOTS)
     w_v = w_in.rearrange("(p j) i -> p j i", j=SLOTS)
     x_v = x.rearrange("b (n p) h w -> b p n (h w)", p=P)
-    dx_v = dx.rearrange("b (m n) h w -> b m n (h w)", n=8)
+    dx_v = dx.rearrange("b (n m) h w -> b m n (h w)", n=8)
     dw_v = dw.rearrange("(m t) i -> m t i", t=SLOTS)
 
     with ExitStack() as ctx:
@@ -38,13 +39,15 @@ def tile_rbfkanhead_v_kernel(
         grp8 = ctx.enter_context(tc.tile_pool(name="grp8", bufs=3))
         raw4 = ctx.enter_context(tc.tile_pool(name="raw4", bufs=2))
         grp4 = ctx.enter_context(tc.tile_pool(name="grp4", bufs=3))
+        zperm = ctx.enter_context(tc.tile_pool(name="zperm", bufs=4))
         zpool = ctx.enter_context(tc.tile_pool(name="zpool", bufs=4))
-        zperm = ctx.enter_context(tc.tile_pool(name="zperm", bufs=3))
-        epool = ctx.enter_context(tc.tile_pool(name="epool", bufs=9))
-        ppool = ctx.enter_context(tc.tile_pool(name="ppool", bufs=9))
-        spool = ctx.enter_context(tc.tile_pool(name="spool", bufs=4))
-        mm = ctx.enter_context(tc.psum_pool(name="mm", bufs=6))
-        acc = ctx.enter_context(tc.psum_pool(name="acc", bufs=2))
+        epool = ctx.enter_context(tc.tile_pool(name="epool", bufs=CFG["e_bufs"]))
+        ppool = ctx.enter_context(tc.tile_pool(name="ppool", bufs=CFG["p_bufs"]))
+        dpool = ctx.enter_context(tc.tile_pool(name="dpool", bufs=CFG["d_bufs"]))
+        spool = ctx.enter_context(tc.tile_pool(name="spool", bufs=6))
+        mm = ctx.enter_context(tc.psum_pool(name="mm", bufs=CFG["mm"]))
+        zbank = ctx.enter_context(tc.psum_pool(name="zbank", bufs=CFG["zb"])) if CFG["zb"] else None
+        acc = ctx.enter_context(tc.psum_pool(name="acc", bufs=CFG["acc"]))
         ctx.enter_context(tc.manual_schedule())
 
         lw_t = keep.tile([P, SLOTS * K], BF16, name="lw_t")
@@ -101,25 +104,32 @@ def tile_rbfkanhead_v_kernel(
 
         nc.vector.tensor_scalar(negc[:], cen_t[:], -1.0, None, ALU.mult)
 
-        z_perm = {}
-
-        def permute_z(engine, g, t):
-            zp = zperm.tile([P, HW], F32, name="zp", tag="zp")
-            dst = zp[:].rearrange("c (j p) -> c j p", j=SLOTS)
-            src = z_raw[g, t][:].rearrange("c (p j) -> c j p", j=SLOTS)
-            if engine is nc.vector:
-                nc.vector.tensor_copy(out=dst, in_=src)
-            else:
-                engine.tensor_scalar(dst, src, 1.0, 1.0, ALU.mult, ALU.mult)
-            z_perm[g, t] = zp
-
-        permute_z(nc.vector, 0, 0)
         nc.vector.scalar_tensor_tensor(wd[:], lw_t[:], 0.0, l1[:], ALU.max, ALU.add)
         nc.vector.tensor_scalar(wd[:], wd[:], 1e-4, None, ALU.add)
         nc.vector.reciprocal(inv[:], wd[:])
         nc.vector.tensor_tensor(sq[:], inv[:], inv[:], ALU.mult)
         nc.vector.tensor_scalar(nsq[:], sq[:], -1.0, None, ALU.mult)
         nc.vector.tensor_scalar(alpha[:], sq[:], -2.0, None, ALU.mult)
+
+        z_bank = {}
+        z_perm = {}
+
+        def permute_z(engine, blk):
+            zp = zperm.tile([P, HW], F32, name="zp", tag="zp")
+            dst = zp[:].rearrange("c (j p) -> c j p", j=SLOTS)
+            src = z_raw[blk // 4, blk % 4][:].rearrange("c (p j) -> c j p", j=SLOTS)
+            if engine is nc.vector:
+                nc.vector.tensor_copy(out=dst, in_=src)
+            else:
+                engine.tensor_scalar(dst, src, 1.0, 1.0, ALU.mult, ALU.mult)
+            z_perm[blk] = zp
+
+        def spread_z(blk):
+            if not CFG["zb"]:
+                return
+            bank = zbank.tile([P, HW], F32, name="z_bank", tag="z_bank")
+            nc.tensor.matmul(bank[:], ident[:], z_perm[blk][:], start=True, stop=True)
+            z_bank[blk] = bank
 
         def quant(codes, scales, src, fmt):
             nc.vector.quantize_mx(out=codes.bitcast(fmt), scales=scales, in_=src)
@@ -139,8 +149,8 @@ def tile_rbfkanhead_v_kernel(
             gg = grp4.tile([P, HW * SLOTS], BF16, name="gg", tag="grp4", align_bytes=64)
             interleave(
                 engine,
-                gg[:].rearrange("p (b a j) -> p b a j", b=SLOTS, j=SLOTS),
-                g_raw[g][:].rearrange("p j (a b) -> p b a j", b=SLOTS),
+                gg[:].rearrange("p (b a j) -> p a b j", b=SLOTS, j=SLOTS),
+                g_raw[g][:].rearrange("p j (a b) -> p a b j", b=SLOTS),
             )
             g_grp[g] = gg
 
@@ -154,11 +164,12 @@ def tile_rbfkanhead_v_kernel(
         def group_ow(engine, t, q):
             if t not in ow_grp:
                 ow_grp[t] = grp8.tile([P, K, P, SLOTS], BF16, name="ow_grp", tag="grp8", align_bytes=64)
-            interleave(
-                engine,
-                ow_grp[t][:, :, 32 * q : 32 * (q + 1), :],
-                ow_raw[q][:].rearrange("p j (m t k) -> p t k m j", t=SLOTS, k=K)[:, t],
-            )
+            for k0 in (0, 4):
+                interleave(
+                    engine,
+                    ow_grp[t][:, k0 : k0 + 4, 32 * q : 32 * (q + 1), :].rearrange("p k m j -> p m k j"),
+                    ow_raw[q][:].rearrange("p j (m t k) -> p t m k j", t=SLOTS, k=K)[:, t, :, k0 : k0 + 4],
+                )
 
         def quant_ow(t, half):
             if t not in oq:
@@ -178,7 +189,7 @@ def tile_rbfkanhead_v_kernel(
             interleave(
                 engine,
                 w_grp[0][:, n0 : n0 + 2],
-                w_raw[:].rearrange("p j (m n) -> p n m j", n=8)[:, n0 : n0 + 2],
+                w_raw[:].rearrange("p j (n m) -> p n m j", n=8)[:, n0 : n0 + 2],
             )
 
         def quant_w():
@@ -213,13 +224,35 @@ def tile_rbfkanhead_v_kernel(
         def split(n):
             return n // 32, (n // 8) % 4, n % 8
 
+        ds = {}
+
+        def sq_pool(n):
+            return on_pool(n) and n % 8 in CFG["sq_k"] and n >= CFG["sq_from"]
+
         def gauss(n):
             g, t, k = split(n)
             col = t * K + k
             e = epool.tile([P, HW], F32, name="e", tag="e")
-            nc.scalar.activation(e[:], z_perm[g, t][:], ACT.Square, bias=negc[:, col : col + 1])
-            nc.scalar.activation(e[:], e[:], ACT.Exp, scale=nsq[:, col : col + 1])
+            if sq_pool(n):
+                d = dpool.tile([P, HW], F32, name="d", tag="d")
+                nc.gpsimd.tensor_scalar(d[:], z_perm[n // 8][:], negc[:, col : col + 1], 1.0, ALU.add, ALU.mult)
+                nc.gpsimd.tensor_tensor(e[:], d[:], d[:], ALU.mult)
+                ds[n] = d
+            else:
+                nc.scalar.activation(e[:], z_perm[n // 8][:], ACT.Square, bias=negc[:, col : col + 1])
             es[n] = e
+
+        def gauss_exp(n):
+            g, t, k = split(n)
+            col = t * K + k
+            nc.scalar.activation(es[n][:], es[n][:], ACT.Exp, scale=nsq[:, col : col + 1])
+
+        def gauss_run(first, last):
+            for n in range(first, last):
+                gauss(n)
+                if n > first:
+                    gauss_exp(n - 1)
+            gauss_exp(last - 1)
 
         def mx_dphi(n):
             g, t, k = split(n)
@@ -238,9 +271,24 @@ def tile_rbfkanhead_v_kernel(
         def offset(n):
             g, t, k = split(n)
             col = t * K + k
+            if on_pool(n):
+                return
             nc.vector.scalar_tensor_tensor(
-                es[n][:], z_perm[g, t][:], negc[:, col : col + 1], es[n][:], ALU.add, ALU.mult
+                es[n][:], (z_bank if CFG["zb"] else z_perm)[n // 8][:], negc[:, col : col + 1], es[n][:], ALU.add, ALU.mult
             )
+
+        def on_pool(n):
+            return n >= CFG["gr_from"] and n % 8 in CFG["gr_k"]
+
+        def offset_pool(n):
+            g, t, k = split(n)
+            col = t * K + k
+            if n in ds:
+                d = ds[n]
+            else:
+                d = dpool.tile([P, HW], F32, name="d", tag="d")
+                nc.gpsimd.tensor_scalar(d[:], z_perm[n // 8][:], negc[:, col : col + 1], 1.0, ALU.add, ALU.mult)
+            nc.gpsimd.tensor_tensor(es[n][:], d[:], es[n][:], ALU.mult)
 
         def product(n):
             g, t, k = split(n)
@@ -302,9 +350,11 @@ def tile_rbfkanhead_v_kernel(
         def copy_back(g, u, engine):
             if u == 0:
                 dzc[g] = grp4.tile([P, HW * SLOTS], BF16, name="dzc", tag="grp4", align_bytes=64)
+                cq[g] = keep.tile([P, HW], U32, name=f"cq{g}", align_bytes=64)
+                cs[g] = keep.tile([P, HW], U8, name=f"cs{g}", align_bytes=64)
             src = back_bank[g, u][:].rearrange("m t p -> m (t p)").bitcast(BF16)
             src = src.rearrange("m (t p e) -> m p e t", t=SLOTS, e=2)
-            dst = dzc[g][:].rearrange("m (p u e t) -> m u p e t", u=2, e=2, t=SLOTS)[:, u]
+            dst = dzc[g][:].rearrange("m (u p e t) -> m u p e t", u=2, e=2, t=SLOTS)[:, u]
             copy_out(engine, dst, src)
 
         def copy_out(engine, dst, src):
@@ -313,10 +363,9 @@ def tile_rbfkanhead_v_kernel(
             else:
                 nc.scalar.copy(dst, src)
 
-        def quant_c(g):
-            cq[g] = keep.tile([P, HW], U32, name=f"cq{g}", align_bytes=64)
-            cs[g] = keep.tile([P, HW], U8, name=f"cs{g}", align_bytes=64)
-            quant(cq[g][:], cs[g][:], dzc[g][:], E5)
+        def quant_c(g, u):
+            cols = slice(256 * u, 256 * (u + 1))
+            quant(cq[g][:, cols], cs[g][:, cols], dzc[g][:, 1024 * u : 1024 * (u + 1)], E5)
 
         stage = {}
 
@@ -339,7 +388,11 @@ def tile_rbfkanhead_v_kernel(
             if n % 2 == 0:
                 stage["x", g, n // 2] = spool.tile([P, 2, HW], F32, name="stage", tag="stage")
             st = stage["x", g, n // 2]
-            copy_out(engine, st[:, n % 2, :], out_bank["x", g, n][:])
+            copy_out(
+                engine,
+                st[:, n % 2, :].rearrange("i (p u e) -> i p u e", u=2, e=2),
+                out_bank["x", g, n][:].rearrange("i (u p e) -> i p u e", u=2, e=2),
+            )
             if n % 2 == 1:
                 nc.sync.dma_start(out=dx_v[g, :, n - 1 : n + 1, :], in_=st[:])
 
@@ -365,91 +418,118 @@ def tile_rbfkanhead_v_kernel(
             if half == 1:
                 nc.sync.dma_start(out=dw_v[:, t, :], in_=st[:].rearrange("m h i -> m (h i)"))
 
+        V = nc.vector
+        S = nc.scalar
+        G = nc.gpsimd
+        ENG = {"V": V, "S": S, "G": G}
+        permute_z(nc.vector, 0)
+        spread_z(0)
         group_g(nc.vector, 0)
         quant_g(0)
-        for q in range(4):
-            group_ow(nc.vector, 0, q)
-        quant_ow(0, 0)
-        quant_ow(0, 1)
-
         n_steps = 64 // UPS
         pe_turn, pe_mx, vec, sca, gp = {}, {}, {}, {}, {}
 
         def at(table, s, fn, *args):
             table.setdefault(s, []).append((fn, args))
 
-        V = nc.vector
-        S = nc.scalar
-        G = nc.gpsimd
-        at(gp, -1, permute_z, G, 0, 1)
+        def on(e, s, fn, *args):
+            at({"V": vec, "S": sca, "G": gp}[e], s, fn, *args)
+
+        heads = [t for t in (1, 2, 3) if CFG["ow_step"][t] < 0]
         for q in range(4):
-            at(gp, -1, group_ow, G, 1, q)
-        for q in range(4):
-            at(gp, 0, group_ow, G, 2, q)
-        at(gp, 0, permute_z, G, 0, 2)
-        for q in range(4):
-            at(gp, 1, group_ow, G, 3, q)
-        at(gp, 1, permute_z, G, 0, 3)
-        at(gp, 1, load_x, 0)
-        at(gp, 2, group_g, G, 1)
+            group_ow(nc.vector, 0, q)
+            if q < 3:
+                for t in heads:
+                    group_ow(V, t, q)
+        quant_ow(0, 0)
+        quant_ow(0, 1)
+        for t in heads:
+            at(vec, 0, group_ow, V, t, 3)
+        for t in (1, 2, 3):
+            if t not in heads:
+                e = CFG["ow_eng"][t]
+                for q in range(4):
+                    on(e, CFG["ow_step"][t] + q // CFG["ow_per"], group_ow, ENG[e], t, q)
+            at(vec, CFG["oq_step"][t], quant_ow, t, 0)
+            at(vec, CFG["oq_step"][t], quant_ow, t, 1)
+        for blk in range(1, 8):
+            at(gp, max(-1, 2 * blk - CFG["zp_lead"]), permute_z, ENG[CFG["zp_eng"]], blk)
+            at(pe_turn, 2 * blk - 2, spread_z, blk)
         for t in range(4):
-            at(gp, 2 + t, load_z, 1, t)
+            at(gp, 1 + t, load_z, 1, t)
+        at(gp, CFG["x_load"], load_x, 0)
+        at(gp, CFG["x_load"], load_x, 1)
+        on(CFG["g1_eng"], CFG["g1_step"], group_g, ENG[CFG["g1_eng"]], 1)
+        at(vec, CFG["gq1_step"], quant_g, 1)
         for n0 in range(4):
-            at(gp, 3 + n0 // 2, group_w, G, 2 * n0)
-        at(gp, 3, load_x, 1)
-        at(gp, 5, permute_z, G, 1, 0)
-        at(gp, 7, permute_z, G, 1, 1)
-        at(gp, 9, permute_z, G, 1, 2)
-        at(gp, 11, permute_z, G, 1, 3)
-        for t in range(1, 4):
-            at(vec, 2 * t - 1, quant_ow, t, 0)
-            at(vec, 2 * t - 1, quant_ow, t, 1)
-        at(vec, 6, quant_g, 1)
-        at(vec, 6, quant_w)
+            on(CFG["w_eng"], CFG["w_step"] + n0 // 2, group_w, ENG[CFG["w_eng"]], 2 * n0)
+        at(vec, CFG["wq_step"], quant_w)
         for i in range(8):
-            at(pe_turn, 3 + i, turn_x, i)
-            at(sca, 5 + i, copy_x, i, S)
+            at(pe_turn, CFG["x_step"] + i, turn_x, i)
+            on(CFG["x_eng"], CFG["x_step"] + i + (1 if CFG["x_eng"] == "S" else 0), copy_x, i, ENG[CFG["x_eng"]])
             if i % 2 == 1:
-                at(vec, 5 + i, quant_x, i // 2)
+                at(vec, CFG["x_step"] + i + 1, quant_x, i // 2)
         for blk in range(7):
-            at(sca, 2 * blk + 4, finish, blk, S)
+            e = CFG["fin_eng"]
+            on(e, 2 * blk + (3 if e == "S" else 2), finish, blk, ENG[e])
             at(vec, 2 * blk + 4, quant_t, blk)
-        at(pe_turn, 10, turn_back, 0, range(4))
-        at(sca, 12, copy_back, 0, 0, S)
-        at(sca, 12, copy_back, 0, 1, S)
-        at(vec, 12, quant_c, 0)
-        for n in range(8):
-            at(pe_mx, 13 + n // 3, mx_dx, 0, n)
-            at(sca, 15 + n // 3, copy_dx, 0, n, S)
+        at(pe_turn, CFG["back"], turn_back, 0, range(4))
+        for u in range(2):
+            e = CFG["back_eng"]
+            on(e, CFG["back"] + 1, copy_back, 0, u, ENG[e])
+            at(vec, CFG["back"] + 2, quant_c, 0, u)
+        late_dx = list(range(8 - CFG["defer"], 8))
+        for n in range(8 - CFG["defer"]):
+            s = CFG["dx_step"] + n // CFG["dx_per"]
+            e = CFG["dx_eng"][n % len(CFG["dx_eng"])]
+            at(pe_mx, s, mx_dx, 0, n)
+            on(e, s + (1 if e == "S" else CFG["dx_v"]), copy_dx, 0, n, ENG[e])
         for t in range(2):
             for half in range(2):
-                at(pe_mx, 13 + 2 * t, mx_dw, t, half)
-                at(sca, 15 + 2 * t, copy_dw, t, half, S)
-        at(pe_mx, 16, turn_back, 1, range(3))
+                s = 13 + 2 * t
+                e = CFG["dw_eng"]
+                at(pe_mx, s, mx_dw, t, half)
+                on(e, s + (1 if e == "S" else CFG["dx_v"]), copy_dw, t, half, ENG[e])
+        at(pe_turn, CFG["back1"], turn_back, 1, range(3))
 
         def run(fns):
             for fn, args in fns:
                 fn(*args)
 
+        def late_pair():
+            pair = late_dx[:2]
+            del_pair = late_dx[2:]
+            late_dx.clear()
+            late_dx.extend(del_pair)
+            for n in pair:
+                mx_dx(0, n)
+            for i, n in enumerate(pair):
+                copy_dx(0, n, S if i == 0 else V)
+
         run(gp.get(-1, []))
         for s in range(n_steps + 1):
-            ahead = list(sca.get(s + 1, []))
             if s == 0:
-                for n in range(2 * UPS):
-                    gauss(n)
+                gauss_run(0, 2 * UPS)
             elif s + 1 < n_steps:
-                for n in range(UPS * (s + 1), UPS * (s + 2)):
-                    gauss(n)
+                gauss_run(UPS * (s + 1), UPS * (s + 2))
             units = range(UPS * s, UPS * (s + 1)) if s < n_steps else range(0)
             for n in units:
                 mx_dphi(n)
-            run(pe_mx.get(s, []))
-            if 0 < s <= n_steps:
+            if CFG["mxo"] == 0:
+                run(pe_mx.get(s, []))
+            if s > 0:
                 for n in range(UPS * (s - 1), UPS * s):
                     sums(n)
+            if CFG["mxo"] == 1:
+                run(pe_mx.get(s, []))
             run(pe_turn.get(s, []))
-            run(ahead)
-            todo = list(vec.get(s, []))
+            run(sca.get(s, []))
+            late = (copy_x, finish, copy_back, copy_dx, copy_dw)
+            todo = [f for f in vec.get(s, []) if f[0] not in late]
+            last = [f for f in vec.get(s, []) if f[0] in late]
+            for n in units:
+                if on_pool(n):
+                    offset_pool(n)
             for n in units:
                 if n == UPS * s:
                     offset(n)
@@ -460,25 +540,31 @@ def tile_rbfkanhead_v_kernel(
                     run(todo[:1])
                     todo = todo[1:]
             run(todo)
+            if s == n_steps:
+                late_pair()
+            run(last)
             run(gp.get(s, []))
 
-        for half in range(2):
-            mx_dw(2, half)
         finish(7, V)
         turn_back(1, (3,))
+        late_pair()
         copy_back(1, 0, S)
         copy_back(1, 1, V)
-        quant_t(7)
         for half in range(2):
-            copy_dw(2, half, S)
-        quant_c(1)
+            mx_dw(2, half)
+        quant_c(1, 0)
+        quant_c(1, 1)
+        late_pair()
+        copy_dw(2, 0, S)
+        mx_dx(1, 0)
+        mx_dx(1, 1)
+        quant_t(7)
+        copy_dw(2, 1, S)
+        for n in range(8):
+            copy_dx(1, n, S if n % 2 == 1 else V)
+            if n + 2 < 8:
+                mx_dx(1, n + 2)
         for half in range(2):
             mx_dw(3, half)
-        copy_dw(3, 0, S)
+        copy_dw(3, 0, V)
         copy_dw(3, 1, S)
-        for n in range(3):
-            mx_dx(1, n)
-        for n in range(8):
-            copy_dx(1, n, V if n % 2 == 0 else S)
-            if n + 3 < 8:
-                mx_dx(1, n + 3)

@@ -18,7 +18,7 @@ FLOPS = 2 * C_OUT * HID * K * B * HW + 2 * 2 * HID * C_IN * B * HW
 P = 128
 SLOTS = 4
 UPS = 4
-CFG = {'gr_from': 16, 'gr_k': (2, 3, 6, 7), 'e_bufs': 12, 'ow_eng': {1: 'S', 2: 'S', 3: 'G'}, 'ow_step': {1: -1, 2: 0, 3: 2}, 'ow_per': 2, 'oq_step': {1: 0, 2: 2, 3: 4}, 'zp_lead': 5, 'zp_eng': 'G', 'x_load': 3, 'g1_eng': 'S', 'g1_step': 4, 'gq1_step': 6, 'w_eng': 'G', 'w_step': 4, 'wq_step': 10, 'x_step': 4, 'x_eng': 'S', 'fin_eng': 'V', 'back': 10, 'back_eng': 'V', 'dx_step': 13, 'dx_per': 3, 'dx_eng': 'S', 'dx_v': 1, 'dw_eng': 'S', 'defer': 0, 'mxo': 1, 'back1': 16, 'sq_k': (), 'sq_from': 16, 'd_bufs': 3, 'p_bufs': 9, 'mm': 5, 'acc': 1, 'zb': 2}
+CFG = {'gr_from': 16, 'gr_k': (2, 6), 'e_bufs': 10, 'ow_eng': {1: 'G', 2: 'S', 3: 'G'}, 'ow_step': {1: -1, 2: 0, 3: 2}, 'ow_per': 2, 'oq_step': {1: 0, 2: 3, 3: 5}, 'zp_lead': 5, 'zp_eng': 'G', 'x_load': 3, 'g1_eng': 'G', 'g1_step': 3, 'gq1_step': 7, 'w_eng': 'G', 'w_step': 7, 'wq_step': 10, 'x_step': 4, 'x_eng': 'S', 'fin_eng': 'V', 'back': 9, 'back_eng': 'S', 'dx_step': 13, 'dx_per': 3, 'dx_eng': 'S', 'dx_v': 0, 'dw_eng': 'V', 'defer': 0, 'mxo': 1, 'back1': 16, 'sq_k': (), 'sq_from': 32, 'd_bufs': 3, 'p_bufs': 6, 'rep': 2, 'pe_run': 2, 'mm': 5, 'acc': 1, 'zb': 2}
 
 
 def tile_rbfkanhead_v_kernel(
@@ -257,15 +257,16 @@ def tile_rbfkanhead_v_kernel(
         def mx_dphi(n):
             g, t, k = split(n)
             bank = mm.tile([P, HW], F32, name="dphi", tag="mm")
-            nc.tensor.matmul_mx(
-                out=bank[:],
-                lhsT=oq[t][:, k * P : (k + 1) * P].bitcast(E4),
-                lhsT_scale=osc[t][:, k * P : (k + 1) * P],
-                rhs=gq[g][:].bitcast(E5),
-                rhs_scale=gs[g][:],
-                start=True,
-                stop=True,
-            )
+            for turn in range(CFG["rep"]):
+                nc.tensor.matmul_mx(
+                    out=bank[:],
+                    lhsT=oq[t][:, k * P : (k + 1) * P].bitcast(E4),
+                    lhsT_scale=osc[t][:, k * P : (k + 1) * P],
+                    rhs=gq[g][:].bitcast(E5),
+                    rhs_scale=gs[g][:],
+                    start=True,
+                    stop=True,
+                )
             dphi[n] = bank
 
         def offset(n):
@@ -513,13 +514,15 @@ def tile_rbfkanhead_v_kernel(
             elif s + 1 < n_steps:
                 gauss_run(UPS * (s + 1), UPS * (s + 2))
             units = range(UPS * s, UPS * (s + 1)) if s < n_steps else range(0)
-            for n in units:
-                mx_dphi(n)
+            for i in range(UPS):
+                n = UPS * s + i
+                if n in units:
+                    mx_dphi(n)
+                if 0 < s and (i + 1) % CFG["pe_run"] == 0:
+                    for j in range(i + 1 - CFG["pe_run"], i + 1):
+                        sums(UPS * (s - 1) + j)
             if CFG["mxo"] == 0:
                 run(pe_mx.get(s, []))
-            if s > 0:
-                for n in range(UPS * (s - 1), UPS * s):
-                    sums(n)
             if CFG["mxo"] == 1:
                 run(pe_mx.get(s, []))
             run(pe_turn.get(s, []))

from contextlib import ExitStack

import concourse.mybir as mybir
from concourse.masks import make_identity

F32 = mybir.dt.float32
BF16 = mybir.dt.bfloat16
U32 = mybir.dt.uint32
U8 = mybir.dt.uint8
E4 = mybir.dt.float8_e4m3fn_x4
E5 = mybir.dt.float8_e5m2_x4
ACT = mybir.ActivationFunctionType
ALU = mybir.AluOpType

B, C_IN, HW, HID, K, C_OUT = 2, 1024, 512, 512, 8, 512
FLOPS = 2 * C_OUT * HID * K * B * HW + 2 * 2 * HID * C_IN * B * HW

P = 128
SLOTS = 4
UPS = 4
CFG = {'gr_from': 16, 'gr_k': (2, 6), 'e_bufs': 10, 'ow_eng': {1: 'G', 2: 'S', 3: 'G'}, 'ow_step': {1: -1, 2: 0, 3: 2}, 'ow_per': 2, 'oq_step': {1: 0, 2: 3, 3: 5}, 'zp_lead': 5, 'zp_eng': 'G', 'x_load': 3, 'g1_eng': 'G', 'g1_step': 3, 'gq1_step': 7, 'w_eng': 'G', 'w_step': 7, 'wq_step': 10, 'x_step': 4, 'x_eng': 'S', 'fin_eng': 'V', 'back': 9, 'back_eng': 'S', 'dx_step': 13, 'dx_per': 3, 'dx_eng': 'S', 'dx_v': 0, 'dw_eng': 'V', 'defer': 0, 'mxo': 1, 'back1': 16, 'sq_k': (), 'sq_from': 32, 'd_bufs': 3, 'p_bufs': 6, 'rep': 2, 'pe_run': 2, 'mm': 5, 'acc': 1, 'zb': 2}


def tile_rbfkanhead_v_kernel(
    tc, x, w_in, b_in, centers, log_widths, out_weight, out_bias, z, grad_out, dx, dw
):
    nc = tc.nc
    z_v = z.rearrange("b (m t) h w -> b m t (h w)", t=SLOTS)
    g_v = grad_out.rearrange("b (p j) h w -> b p j (h w)", j=SLOTS)
    ow_v = out_weight.rearrange("(p j) c k -> p j (c k)", j=SLOTS)
    w_v = w_in.rearrange("(p j) i -> p j i", j=SLOTS)
    x_v = x.rearrange("b (n p) h w -> b p n (h w)", p=P)
    dx_v = dx.rearrange("b (n m) h w -> b m n (h w)", n=8)
    dw_v = dw.rearrange("(m t) i -> m t i", t=SLOTS)

    with ExitStack() as ctx:
        keep = ctx.enter_context(tc.tile_pool(name="keep", bufs=1))
        raw8 = ctx.enter_context(tc.tile_pool(name="raw8", bufs=5))
        grp8 = ctx.enter_context(tc.tile_pool(name="grp8", bufs=3))
        raw4 = ctx.enter_context(tc.tile_pool(name="raw4", bufs=2))
        grp4 = ctx.enter_context(tc.tile_pool(name="grp4", bufs=3))
        zperm = ctx.enter_context(tc.tile_pool(name="zperm", bufs=4))
        zpool = ctx.enter_context(tc.tile_pool(name="zpool", bufs=4))
        epool = ctx.enter_context(tc.tile_pool(name="epool", bufs=CFG["e_bufs"]))
        ppool = ctx.enter_context(tc.tile_pool(name="ppool", bufs=CFG["p_bufs"]))
        dpool = ctx.enter_context(tc.tile_pool(name="dpool", bufs=CFG["d_bufs"]))
        spool = ctx.enter_context(tc.tile_pool(name="spool", bufs=6))
        mm = ctx.enter_context(tc.psum_pool(name="mm", bufs=CFG["mm"]))
        zbank = ctx.enter_context(tc.psum_pool(name="zbank", bufs=CFG["zb"])) if CFG["zb"] else None
        acc = ctx.enter_context(tc.psum_pool(name="acc", bufs=CFG["acc"]))
        ctx.enter_context(tc.manual_schedule())

        lw_t = keep.tile([P, SLOTS * K], BF16, name="lw_t")
        cen_t = keep.tile([P, SLOTS * K], BF16, name="cen_t")
        nc.sync.dma_start(out=lw_t[:], in_=log_widths.rearrange("a (m t) k b c -> m (a t k b c)", t=SLOTS))
        nc.sync.dma_start(out=cen_t[:], in_=centers.rearrange("a (m t) k b c -> m (a t k b c)", t=SLOTS))
        z_raw = {}

        def load_z(g, t):
            zt_ = zpool.tile([P, HW], F32, name="z_raw", tag="z_raw")
            nc.sync.dma_start(out=zt_[:], in_=z_v[g, :, t, :])
            z_raw[g, t] = zt_

        def load_g(g):
            gt_ = raw4.tile([P, SLOTS, HW], BF16, name="g_raw", tag="g_raw")
            nc.sync.dma_start(out=gt_[:], in_=g_v[g])
            return gt_

        load_z(0, 0)
        g_raw = {0: load_g(0)}
        ow_raw = []
        for q in range(4):
            r = raw8.tile([P, SLOTS, 1024], BF16, name="ow_raw", tag="raw8")
            nc.sync.dma_start(out=r[:], in_=ow_v[:, :, 1024 * q : 1024 * (q + 1)])
            ow_raw.append(r)
        load_z(0, 1)
        load_z(0, 2)
        load_z(0, 3)
        w_raw = raw8.tile([P, SLOTS, C_IN], BF16, name="w_raw", tag="raw8")
        nc.sync.dma_start(out=w_raw[:], in_=w_v)
        g_raw[1] = load_g(1)
        x_raw = {}

        def load_x(b):
            xt_ = raw8.tile([P, 8, HW], BF16, name="x_raw", tag="raw8")
            nc.sync.dma_start(out=xt_[:], in_=x_v[b])
            x_raw[b] = xt_

        ident = keep.tile([P, P], F32, name="ident")
        make_identity(nc, ident[:])
        ab = keep.tile([P, SLOTS * K], F32, name="ab")
        ex = keep.tile([P, SLOTS * K], F32, name="ex")
        l1 = keep.tile([P, SLOTS * K], F32, name="l1")
        wd = keep.tile([P, SLOTS * K], F32, name="wd")
        inv = keep.tile([P, SLOTS * K], F32, name="inv")
        sq = keep.tile([P, SLOTS * K], F32, name="sq")
        nsq = keep.tile([P, SLOTS * K], F32, name="nsq")
        alpha = keep.tile([P, SLOTS * K], F32, name="alpha")
        negc = keep.tile([P, SLOTS * K], F32, name="negc")

        nc.scalar.activation(ab[:], lw_t[:], ACT.Abs)
        nc.scalar.activation(ex[:], ab[:], ACT.Exp, scale=-1.0)
        nc.scalar.activation(l1[:], ex[:], ACT.Ln, bias=1.0)

        nc.vector.tensor_scalar(negc[:], cen_t[:], -1.0, None, ALU.mult)

        nc.vector.scalar_tensor_tensor(wd[:], lw_t[:], 0.0, l1[:], ALU.max, ALU.add)
        nc.vector.tensor_scalar(wd[:], wd[:], 1e-4, None, ALU.add)
        nc.vector.reciprocal(inv[:], wd[:])
        nc.vector.tensor_tensor(sq[:], inv[:], inv[:], ALU.mult)
        nc.vector.tensor_scalar(nsq[:], sq[:], -1.0, None, ALU.mult)
        nc.vector.tensor_scalar(alpha[:], sq[:], -2.0, None, ALU.mult)

        z_bank = {}
        z_perm = {}

        def permute_z(engine, blk):
            zp = zperm.tile([P, HW], F32, name="zp", tag="zp")
            dst = zp[:].rearrange("c (j p) -> c j p", j=SLOTS)
            src = z_raw[blk // 4, blk % 4][:].rearrange("c (p j) -> c j p", j=SLOTS)
            if engine is nc.vector:
                nc.vector.tensor_copy(out=dst, in_=src)
            else:
                engine.tensor_scalar(dst, src, 1.0, 1.0, ALU.mult, ALU.mult)
            z_perm[blk] = zp

        def spread_z(blk):
            if not CFG["zb"]:
                return
            bank = zbank.tile([P, HW], F32, name="z_bank", tag="z_bank")
            nc.tensor.matmul(bank[:], ident[:], z_perm[blk][:], start=True, stop=True)
            z_bank[blk] = bank

        def quant(codes, scales, src, fmt):
            nc.vector.quantize_mx(out=codes.bitcast(fmt), scales=scales, in_=src)

        def interleave(engine, dst, src):
            if engine is nc.vector:
                nc.vector.tensor_copy(out=dst, in_=src)
            elif engine is nc.scalar:
                nc.scalar.copy(dst, src)
            else:
                engine.tensor_scalar(dst, src, 1.0, 1.0, ALU.mult, ALU.mult)

        gq, gs = {}, {}
        g_grp = {}

        def group_g(engine, g):
            gg = grp4.tile([P, HW * SLOTS], BF16, name="gg", tag="grp4", align_bytes=64)
            interleave(
                engine,
                gg[:].rearrange("p (b a j) -> p a b j", b=SLOTS, j=SLOTS),
                g_raw[g][:].rearrange("p j (a b) -> p a b j", b=SLOTS),
            )
            g_grp[g] = gg

        def quant_g(g):
            gq[g] = keep.tile([P, HW], U32, name=f"gq{g}", align_bytes=64)
            gs[g] = keep.tile([P, HW], U8, name=f"gs{g}", align_bytes=64)
            quant(gq[g][:], gs[g][:], g_grp[g][:], E5)

        ow_grp, oq, osc = {}, {}, {}

        def group_ow(engine, t, q):
            if t not in ow_grp:
                ow_grp[t] = grp8.tile([P, K, P, SLOTS], BF16, name="ow_grp", tag="grp8", align_bytes=64)
            for k0 in (0, 4):
                interleave(
                    engine,
                    ow_grp[t][:, k0 : k0 + 4, 32 * q : 32 * (q + 1), :].rearrange("p k m j -> p m k j"),
                    ow_raw[q][:].rearrange("p j (m t k) -> p t m k j", t=SLOTS, k=K)[:, t, :, k0 : k0 + 4],
                )

        def quant_ow(t, half):
            if t not in oq:
                oq[t] = keep.tile([P, K * P], U32, name=f"oq{t}", align_bytes=64)
                osc[t] = keep.tile([P, K * P], U8, name=f"os{t}", align_bytes=64)
            cols = slice(half * 512, half * 512 + 512)
            src = ow_grp[t][:].rearrange("p k m j -> p (k m j)")[:, half * 2048 : half * 2048 + 2048]
            quant(oq[t][:, cols], osc[t][:, cols], src, E4)

        w_grp = {}
        wq = keep.tile([P, C_IN], U32, name="wq", align_bytes=64)
        ws = keep.tile([P, C_IN], U8, name="ws", align_bytes=64)

        def group_w(engine, n0):
            if 0 not in w_grp:
                w_grp[0] = grp8.tile([P, 8, P, SLOTS], BF16, name="w_grp", tag="grp8", align_bytes=64)
            interleave(
                engine,
                w_grp[0][:, n0 : n0 + 2],
                w_raw[:].rearrange("p j (n m) -> p n m j", n=8)[:, n0 : n0 + 2],
            )

        def quant_w():
            quant(wq[:], ws[:], w_grp[0][:].rearrange("p n m j -> p (n m j)"), E4)

        xq = {b: keep.tile([P, C_IN], U32, name=f"xq{b}", align_bytes=64) for b in range(B)}
        xs = {b: keep.tile([P, C_IN], U8, name=f"xs{b}", align_bytes=64) for b in range(B)}
        x_grp, x_bank = {}, {}

        def turn_x(i):
            b, q = i // 4, i % 4
            bank = mm.tile([P, 2, 256], F32, name="x_bank", tag="mm")
            for a in range(2):
                words = x_raw[b][:, 2 * q + a, :].bitcast(F32).rearrange("i (p u) -> i p u", u=2)
                for u in range(2):
                    nc.tensor.transpose(bank[:, u, P * a : P * (a + 1)], words[:, :, u], ident[:])
            x_bank[i] = bank

        def copy_x(i, engine):
            if i % 2 == 0:
                x_grp[i // 2] = grp4.tile([P, 512 * SLOTS], BF16, name="x_grp", tag="grp4", align_bytes=64)
            dst = x_grp[i // 2][:, 1024 * (i % 2) : 1024 * (i % 2 + 1)].bitcast(F32)
            copy_out(engine, dst.rearrange("p (i u) -> p i u", u=2), x_bank[i][:].rearrange("p u i -> p i u"))

        def quant_x(i):
            b, half = i // 2, i % 2
            cols = slice(512 * half, 512 * (half + 1))
            quant(xq[b][:, cols], xs[b][:, cols], x_grp[i][:], E4)

        es, ps, qs, dphi = {}, {}, {}, {}

        def split(n):
            return n // 32, (n // 8) % 4, n % 8

        ds = {}

        def sq_pool(n):
            return on_pool(n) and n % 8 in CFG["sq_k"] and n >= CFG["sq_from"]

        def gauss(n):
            g, t, k = split(n)
            col = t * K + k
            e = epool.tile([P, HW], F32, name="e", tag="e")
            if sq_pool(n):
                d = dpool.tile([P, HW], F32, name="d", tag="d")
                nc.gpsimd.tensor_scalar(d[:], z_perm[n // 8][:], negc[:, col : col + 1], 1.0, ALU.add, ALU.mult)
                nc.gpsimd.tensor_tensor(e[:], d[:], d[:], ALU.mult)
                ds[n] = d
            else:
                nc.scalar.activation(e[:], z_perm[n // 8][:], ACT.Square, bias=negc[:, col : col + 1])
            es[n] = e

        def gauss_exp(n):
            g, t, k = split(n)
            col = t * K + k
            nc.scalar.activation(es[n][:], es[n][:], ACT.Exp, scale=nsq[:, col : col + 1])

        def gauss_run(first, last):
            for n in range(first, last):
                gauss(n)
                if n > first:
                    gauss_exp(n - 1)
            gauss_exp(last - 1)

        def mx_dphi(n):
            g, t, k = split(n)
            bank = mm.tile([P, HW], F32, name="dphi", tag="mm")
            for turn in range(CFG["rep"]):
                nc.tensor.matmul_mx(
                    out=bank[:],
                    lhsT=oq[t][:, k * P : (k + 1) * P].bitcast(E4),
                    lhsT_scale=osc[t][:, k * P : (k + 1) * P],
                    rhs=gq[g][:].bitcast(E5),
                    rhs_scale=gs[g][:],
                    start=True,
                    stop=True,
                )
            dphi[n] = bank

        def offset(n):
            g, t, k = split(n)
            col = t * K + k
            if on_pool(n):
                return
            nc.vector.scalar_tensor_tensor(
                es[n][:], (z_bank if CFG["zb"] else z_perm)[n // 8][:], negc[:, col : col + 1], es[n][:], ALU.add, ALU.mult
            )

        def on_pool(n):
            return n >= CFG["gr_from"] and n % 8 in CFG["gr_k"]

        def offset_pool(n):
            g, t, k = split(n)
            col = t * K + k
            if n in ds:
                d = ds[n]
            else:
                d = dpool.tile([P, HW], F32, name="d", tag="d")
                nc.gpsimd.tensor_scalar(d[:], z_perm[n // 8][:], negc[:, col : col + 1], 1.0, ALU.add, ALU.mult)
            nc.gpsimd.tensor_tensor(es[n][:], d[:], es[n][:], ALU.mult)

        def product(n):
            g, t, k = split(n)
            col = t * K + k
            p = ppool.tile([P, HW], F32, name="p", tag="p")
            nc.vector.scalar_tensor_tensor(
                p[:], dphi[n][:], alpha[:, col : col + 1], es[n][:], ALU.mult, ALU.mult
            )
            ps[n] = p

        bank2 = {}

        def add_turned(bank, src, first, last):
            for j in range(SLOTS):
                nc.tensor.matmul(
                    bank[:, j, :],
                    src[:, P * j : P * (j + 1)],
                    ident[:],
                    start=first and j == 0,
                    stop=last and j == SLOTS - 1,
                    is_transpose=True,
                )

        def sums(n):
            g, t, k = split(n)
            blk = n // 8
            if k == 0:
                bank2[blk] = acc.tile([P, SLOTS, P], F32, name="bank2", tag="bank2")
            add_turned(bank2[blk], ps[n], k == 0, k == K - 1)


        dz = {}
        tq = {b: keep.tile([P, SLOTS * P], U32, name=f"tq{b}", align_bytes=64) for b in range(B)}
        tsc = {b: keep.tile([P, SLOTS * P], U8, name=f"tsc{b}", align_bytes=64) for b in range(B)}
        for b in range(B):
            dz[b] = keep.tile([P, SLOTS, P * SLOTS], BF16, name=f"dz{b}", align_bytes=64)

        def finish(blk, engine):
            dst = dz[blk // 4][:, blk % 4, :].rearrange("p (m j) -> p m j", j=SLOTS)
            copy_out(engine, dst, bank2[blk][:].rearrange("p j m -> p m j"))

        def quant_t(blk):
            g, t = blk // 4, blk % 4
            cols = slice(P * t, P * (t + 1))
            quant(tq[g][:, cols], tsc[g][:, cols], dz[g][:, t, :], E5)

        back_bank = {}

        def turn_back(g, ts):
            for u in range(2):
                if (g, u) not in back_bank:
                    back_bank[g, u] = mm.tile([P, SLOTS, P], F32, name="back", tag="mm")
                for t in ts:
                    words = dz[g][:, t, :].bitcast(F32).rearrange("p (m u) -> p m u", u=2)
                    nc.tensor.transpose(back_bank[g, u][:, t, :], words[:, :, u], ident[:])

        dzc, cq, cs = {}, {}, {}

        def copy_back(g, u, engine):
            if u == 0:
                dzc[g] = grp4.tile([P, HW * SLOTS], BF16, name="dzc", tag="grp4", align_bytes=64)
                cq[g] = keep.tile([P, HW], U32, name=f"cq{g}", align_bytes=64)
                cs[g] = keep.tile([P, HW], U8, name=f"cs{g}", align_bytes=64)
            src = back_bank[g, u][:].rearrange("m t p -> m (t p)").bitcast(BF16)
            src = src.rearrange("m (t p e) -> m p e t", t=SLOTS, e=2)
            dst = dzc[g][:].rearrange("m (u p e t) -> m u p e t", u=2, e=2, t=SLOTS)[:, u]
            copy_out(engine, dst, src)

        def copy_out(engine, dst, src):
            if engine is nc.vector:
                nc.vector.tensor_copy(out=dst, in_=src)
            else:
                nc.scalar.copy(dst, src)

        def quant_c(g, u):
            cols = slice(256 * u, 256 * (u + 1))
            quant(cq[g][:, cols], cs[g][:, cols], dzc[g][:, 1024 * u : 1024 * (u + 1)], E5)

        stage = {}

        out_bank = {}

        def mx_dx(g, n):
            bank = mm.tile([P, HW], F32, name="dx_bank", tag="mm")
            nc.tensor.matmul_mx(
                out=bank[:],
                lhsT=wq[:, P * n : P * (n + 1)].bitcast(E4),
                lhsT_scale=ws[:, P * n : P * (n + 1)],
                rhs=cq[g][:].bitcast(E5),
                rhs_scale=cs[g][:],
                start=True,
                stop=True,
            )
            out_bank["x", g, n] = bank

        def copy_dx(g, n, engine):
            if n % 2 == 0:
                stage["x", g, n // 2] = spool.tile([P, 2, HW], F32, name="stage", tag="stage")
            st = stage["x", g, n // 2]
            copy_out(
                engine,
                st[:, n % 2, :].rearrange("i (p u e) -> i p u e", u=2, e=2),
                out_bank["x", g, n][:].rearrange("i (u p e) -> i p u e", u=2, e=2),
            )
            if n % 2 == 1:
                nc.sync.dma_start(out=dx_v[g, :, n - 1 : n + 1, :], in_=st[:])

        def mx_dw(t, half):
            bank = mm.tile([P, 512], F32, name="dw_bank", tag="mm")
            for g in range(B):
                nc.tensor.matmul_mx(
                    out=bank[:],
                    lhsT=tq[g][:, P * t : P * (t + 1)].bitcast(E5),
                    lhsT_scale=tsc[g][:, P * t : P * (t + 1)],
                    rhs=xq[g][:, 512 * half : 512 * (half + 1)].bitcast(E4),
                    rhs_scale=xs[g][:, 512 * half : 512 * (half + 1)],
                    start=g == 0,
                    stop=g == B - 1,
                )
            out_bank["w", t, half] = bank

        def copy_dw(t, half, engine):
            if half == 0:
                stage["w", t] = spool.tile([P, 2, 512], F32, name="stage", tag="stage")
            st = stage["w", t]
            copy_out(engine, st[:, half, :], out_bank["w", t, half][:])
            if half == 1:
                nc.sync.dma_start(out=dw_v[:, t, :], in_=st[:].rearrange("m h i -> m (h i)"))

        V = nc.vector
        S = nc.scalar
        G = nc.gpsimd
        ENG = {"V": V, "S": S, "G": G}
        permute_z(nc.vector, 0)
        spread_z(0)
        group_g(nc.vector, 0)
        quant_g(0)
        n_steps = 64 // UPS
        pe_turn, pe_mx, vec, sca, gp = {}, {}, {}, {}, {}

        def at(table, s, fn, *args):
            table.setdefault(s, []).append((fn, args))

        def on(e, s, fn, *args):
            at({"V": vec, "S": sca, "G": gp}[e], s, fn, *args)

        heads = [t for t in (1, 2, 3) if CFG["ow_step"][t] < 0]
        for q in range(4):
            group_ow(nc.vector, 0, q)
            if q < 3:
                for t in heads:
                    group_ow(V, t, q)
        quant_ow(0, 0)
        quant_ow(0, 1)
        for t in heads:
            at(vec, 0, group_ow, V, t, 3)
        for t in (1, 2, 3):
            if t not in heads:
                e = CFG["ow_eng"][t]
                for q in range(4):
                    on(e, CFG["ow_step"][t] + q // CFG["ow_per"], group_ow, ENG[e], t, q)
            at(vec, CFG["oq_step"][t], quant_ow, t, 0)
            at(vec, CFG["oq_step"][t], quant_ow, t, 1)
        for blk in range(1, 8):
            at(gp, max(-1, 2 * blk - CFG["zp_lead"]), permute_z, ENG[CFG["zp_eng"]], blk)
            at(pe_turn, 2 * blk - 2, spread_z, blk)
        for t in range(4):
            at(gp, 1 + t, load_z, 1, t)
        at(gp, CFG["x_load"], load_x, 0)
        at(gp, CFG["x_load"], load_x, 1)
        on(CFG["g1_eng"], CFG["g1_step"], group_g, ENG[CFG["g1_eng"]], 1)
        at(vec, CFG["gq1_step"], quant_g, 1)
        for n0 in range(4):
            on(CFG["w_eng"], CFG["w_step"] + n0 // 2, group_w, ENG[CFG["w_eng"]], 2 * n0)
        at(vec, CFG["wq_step"], quant_w)
        for i in range(8):
            at(pe_turn, CFG["x_step"] + i, turn_x, i)
            on(CFG["x_eng"], CFG["x_step"] + i + (1 if CFG["x_eng"] == "S" else 0), copy_x, i, ENG[CFG["x_eng"]])
            if i % 2 == 1:
                at(vec, CFG["x_step"] + i + 1, quant_x, i // 2)
        for blk in range(7):
            e = CFG["fin_eng"]
            on(e, 2 * blk + (3 if e == "S" else 2), finish, blk, ENG[e])
            at(vec, 2 * blk + 4, quant_t, blk)
        at(pe_turn, CFG["back"], turn_back, 0, range(4))
        for u in range(2):
            e = CFG["back_eng"]
            on(e, CFG["back"] + 1, copy_back, 0, u, ENG[e])
            at(vec, CFG["back"] + 2, quant_c, 0, u)
        late_dx = list(range(8 - CFG["defer"], 8))
        for n in range(8 - CFG["defer"]):
            s = CFG["dx_step"] + n // CFG["dx_per"]
            e = CFG["dx_eng"][n % len(CFG["dx_eng"])]
            at(pe_mx, s, mx_dx, 0, n)
            on(e, s + (1 if e == "S" else CFG["dx_v"]), copy_dx, 0, n, ENG[e])
        for t in range(2):
            for half in range(2):
                s = 13 + 2 * t
                e = CFG["dw_eng"]
                at(pe_mx, s, mx_dw, t, half)
                on(e, s + (1 if e == "S" else CFG["dx_v"]), copy_dw, t, half, ENG[e])
        at(pe_turn, CFG["back1"], turn_back, 1, range(3))

        def run(fns):
            for fn, args in fns:
                fn(*args)

        def late_pair():
            pair = late_dx[:2]
            del_pair = late_dx[2:]
            late_dx.clear()
            late_dx.extend(del_pair)
            for n in pair:
                mx_dx(0, n)
            for i, n in enumerate(pair):
                copy_dx(0, n, S if i == 0 else V)

        run(gp.get(-1, []))
        for s in range(n_steps + 1):
            if s == 0:
                gauss_run(0, 2 * UPS)
            elif s + 1 < n_steps:
                gauss_run(UPS * (s + 1), UPS * (s + 2))
            units = range(UPS * s, UPS * (s + 1)) if s < n_steps else range(0)
            for i in range(UPS):
                n = UPS * s + i
                if n in units:
                    mx_dphi(n)
                if 0 < s and (i + 1) % CFG["pe_run"] == 0:
                    for j in range(i + 1 - CFG["pe_run"], i + 1):
                        sums(UPS * (s - 1) + j)
            if CFG["mxo"] == 0:
                run(pe_mx.get(s, []))
            if CFG["mxo"] == 1:
                run(pe_mx.get(s, []))
            run(pe_turn.get(s, []))
            run(sca.get(s, []))
            late = (copy_x, finish, copy_back, copy_dx, copy_dw)
            todo = [f for f in vec.get(s, []) if f[0] not in late]
            last = [f for f in vec.get(s, []) if f[0] in late]
            for n in units:
                if on_pool(n):
                    offset_pool(n)
            for n in units:
                if n == UPS * s:
                    offset(n)
                if n + 1 in units:
                    offset(n + 1)
                product(n)
                if len(todo) > 0:
                    run(todo[:1])
                    todo = todo[1:]
            run(todo)
            if s == n_steps:
                late_pair()
            run(last)
            run(gp.get(s, []))

        finish(7, V)
        turn_back(1, (3,))
        late_pair()
        copy_back(1, 0, S)
        copy_back(1, 1, V)
        for half in range(2):
            mx_dw(2, half)
        quant_c(1, 0)
        quant_c(1, 1)
        late_pair()
        copy_dw(2, 0, S)
        mx_dx(1, 0)
        mx_dx(1, 1)
        quant_t(7)
        copy_dw(2, 1, S)
        for n in range(8):
            copy_dx(1, n, S if n % 2 == 1 else V)
            if n + 2 < 8:
                mx_dx(1, n + 2)
        for half in range(2):
            mx_dw(3, half)
        copy_dw(3, 0, V)
        copy_dw(3, 1, S)
